import numpy as np
import ml_dtypes


def mxq(x, axis, fmt="e4m3"):
    dtype, down = {"e4m3": (ml_dtypes.float8_e4m3fn, 7), "e5m2": (ml_dtypes.float8_e5m2, 14)}[fmt]
    v = np.moveaxis(np.asarray(x, np.float32).astype(ml_dtypes.bfloat16).astype(np.float64), axis, -1)
    blocks = v.reshape(v.shape[:-1] + (-1, 32))
    amax = np.abs(blocks).max(-1, keepdims=True)
    byte = np.maximum(np.where(amax > 0, np.frexp(amax)[1] - 1 + 127, 0) - down, 1)
    scale = np.exp2(byte - 127.0)
    codes = (blocks / scale).astype(np.float32).astype(dtype).astype(np.float64)
    return np.moveaxis((codes * scale).reshape(v.shape), -1, axis)


WIDE = False


def mx_kscale(k):
    if not WIDE:
        return np.ones(k)
    levels = np.array([10, -10, 5, -5, 0])
    a = np.random.permutation(np.resize(levels, k // 512 * 4)).reshape(k // 512, 4)
    idx = np.arange(k)
    return np.exp2(a[idx // 512, idx % 128 // 32])


BF16 = ml_dtypes.bfloat16


def bf(x):
    return np.asarray(x, np.float32).astype(BF16)


def f64(x):
    return np.asarray(x).astype(np.float64)


B, S, IN_F, OUT_F, GROUP_SIZE = 4, 256, 2048, 2048, 32


def group_factors():
    u = np.unique(mx_kscale(IN_F))
    order = np.stack([u[::-1], u], 1).ravel()[:len(u)]
    return order[np.arange(IN_F // GROUP_SIZE) % len(u)]


def setup_inputs():
    g = group_factors()
    s = np.repeat(g, GROUP_SIZE)
    x = np.random.standard_normal((B, S, IN_F)) * s
    sw = np.random.standard_normal((OUT_F, IN_F))
    sw = np.where(sw == 0, 1.0, sw)
    scales = np.random.uniform(0.32, 3.2, OUT_F * IN_F // GROUP_SIZE) / np.sqrt(IN_F) / np.tile(g, OUT_F)
    return {"x": bf(x), "sign_weights": bf(sw), "scales": bf(scales)}


def reference(x, sign_weights, scales):
    binary = np.sign(f64(sign_weights))
    scale_mat = np.repeat(f64(scales), GROUP_SIZE).reshape(OUT_F, IN_F)
    weight = binary * scale_mat
    return mxq(f64(x), 2, "e4m3") @ mxq(weight, 1, "e4m3").T

@@ -1,0 +1,258 @@
+from contextlib import ExitStack
+
+import concourse.mybir as mybir
+from concourse.masks import make_identity
+
+F32 = mybir.dt.float32
+BF16 = mybir.dt.bfloat16
+U32 = mybir.dt.uint32
+U8 = mybir.dt.uint8
+FP8X4 = mybir.dt.float8_e4m3fn_x4
+ALU = mybir.AluOpType
+
+P = 128
+M = 1024
+K = 2048
+O = 2048
+FLOPS = 2 * M * K * O
+
+PINNED = True
+
+TINY = 2.0 ** -126
+AMP = 2.0 ** 7
+BACK = 2.0 ** 126
+
+
+def tile_stebitlinear_kernel(tc, x, sign_weights, scales, out):
+    nc = tc.nc
+    xf = x.flatten_outer_dims()
+    of = out.flatten_outer_dims()
+    with ExitStack() as ctx:
+        keep = ctx.enter_context(tc.tile_pool(name="keep", bufs=1))
+        work = ctx.enter_context(tc.tile_pool(name="work", bufs=2))
+        psum_t = ctx.enter_context(tc.psum_pool(name="psum_t", bufs=4))
+        psum_m = ctx.enter_context(tc.psum_pool(name="psum_m", bufs=4))
+
+        ident = keep.tile([P, P], F32, name="ident")
+        make_identity(nc, ident[:])
+        sc_raw = keep.tile([P, 16 * 64], BF16, name="sc_raw")
+        sc2 = keep.tile([P, 16 * 64, 2], BF16, name="sc2")
+        xq = keep.tile([P, 8, 512], U32, name="xq", align_bytes=64)
+        xs = keep.tile([P, 8, 512], U8, name="xs", align_bytes=64)
+        wq = keep.tile([P, 8, 4, 256], U32, name="wq", align_bytes=64)
+        ws = keep.tile([P, 8, 4, 256], U8, name="ws", align_bytes=64)
+
+        if PINNED:
+            ctx.enter_context(tc.manual_schedule())
+
+        st = {}
+
+        def load_scales():
+            nc.sync.dma_start(
+                out=sc_raw[:].rearrange("p (t g) -> p t g", g=64),
+                in_=scales.rearrange("(t p g) -> p t g", p=P, g=64),
+            )
+
+        def dup(t0, t1):
+            n = (t1 - t0) * 64
+            nc.scalar.copy(
+                out=sc2[:, t0 * 64 : t1 * 64, :],
+                in_=sc_raw[:, t0 * 64 : t1 * 64].unsqueeze(2).to_broadcast([P, n, 2]),
+            )
+
+        def load_w(t):
+            j = t // 2
+            if ("swp", j) not in st:
+                st[("swp", j)] = work.tile([P, 2, K], BF16, name="swp", tag="swp", bufs=5)
+            nc.sync.dma_start(out=st[("swp", j)][:, t % 2, :], in_=sign_weights[t * P : (t + 1) * P, :])
+
+        def load_x(i):
+            j = i // 2
+            if ("xr", j) not in st:
+                st[("xr", j)] = work.tile([P, 2, K], BF16, name="xr", tag="xr", bufs=4)
+            nc.sync.dma_start(out=st[("xr", j)][:, i % 2, :], in_=xf[i * P : (i + 1) * P, :])
+
+        def sign_v(ts):
+            swp = st[("swp", ts[0] // 2)]
+            if len(ts) == 2:
+                v = swp[:].rearrange("p t k -> p (t k)")
+            else:
+                v = swp[:, ts[0] % 2, :]
+            nc.vector.tensor_scalar(out=v, in0=v, scalar1=AMP, scalar2=TINY, op0=ALU.mult, op1=ALU.min)
+            nc.vector.tensor_scalar(out=v, in0=v, scalar1=-TINY, scalar2=BACK, op0=ALU.max, op1=ALU.mult)
+
+        def mult(t):
+            j = t // 2
+            if ("wsr", j) not in st:
+                st[("wsr", j)] = work.tile([P, 2 * K], BF16, name="wsr", tag="wsr", bufs=2)
+            wsr = st[("wsr", j)]
+            nc.vector.tensor_tensor(
+                out=wsr[:].rearrange("p (t u q e) -> p t q u e", t=2, u=2, q=512, e=2)[:, t % 2],
+                in0=st[("swp", j)][:, t % 2, :],
+                in1=sc2[:, t * 64 : (t + 1) * 64, :].unsqueeze(2).to_broadcast([P, 64, 16, 2]),
+                op=ALU.mult,
+            )
+
+        def trans_w(t):
+            words = st[("wsr", t // 2)][:].bitcast(F32).rearrange("p (t u c q) -> p t u c q", t=2, u=2, c=4)
+            for h in range(2):
+                tp = psum_t.tile([P, 2, 2, P], F32, name="tp", tag="tp")
+                st[("tpw", t, h)] = tp
+                for cc in range(2):
+                    for u in range(2):
+                        nc.tensor.transpose(tp[:, cc, u, :], words[:, t % 2, u, 2 * h + cc, :], ident[:])
+
+        def exit_w(t):
+            j = t // 2
+            if ("wg", j) not in st:
+                st[("wg", j)] = work.tile([P, 2 * K], BF16, name="wg", tag="wg", bufs=2, align_bytes=64)
+            words = st[("wg", j)][:].bitcast(F32).rearrange("p (c o u) -> p c o u", c=4, u=2)
+            o0 = (t % 2) * P
+            for h in range(2):
+                nc.scalar.copy(
+                    out=words[:, 2 * h : 2 * h + 2, o0 : o0 + P, :],
+                    in_=st[("tpw", t, h)][:].rearrange("p c u m -> p c m u"),
+                )
+
+        def quant_w(j):
+            wg = st[("wg", j)]
+            for c in range(4):
+                nc.vector.quantize_mx(
+                    out=wq[:, j, c, :].bitcast(FP8X4),
+                    scales=ws[:, j, c, :],
+                    in_=wg[:, c * 1024 : (c + 1) * 1024],
+                )
+
+        def trans_x(i):
+            words = st[("xr", i // 2)][:].bitcast(F32).rearrange("p t (c q u) -> p t c u q", c=4, u=2)
+            for h in range(2):
+                tp = psum_t.tile([P, 2, 2, P], F32, name="tp", tag="tp")
+                st[("tpx", i, h)] = tp
+                for cc in range(2):
+                    for u in range(2):
+                        nc.tensor.transpose(tp[:, cc, u, :], words[:, i % 2, 2 * h + cc, u, :], ident[:])
+
+        def exit_x(i):
+            xg = work.tile([P, K], BF16, name="xg", tag="xg", bufs=4, align_bytes=64)
+            st[("xg", i)] = xg
+            words = xg[:].bitcast(F32).rearrange("p (c m u) -> p c m u", c=4, u=2)
+            for h in range(2):
+                nc.scalar.copy(
+                    out=words[:, 2 * h : 2 * h + 2, :, :],
+                    in_=st[("tpx", i, h)][:].rearrange("p c u m -> p c m u"),
+                )
+
+        def quant_x(i):
+            nc.vector.quantize_mx(out=xq[:, i, :].bitcast(FP8X4), scales=xs[:, i, :], in_=st[("xg", i)][:])
+
+        def mx_bank(j, b):
+            acc = psum_m.tile([P, 2, 256], F32, name="acc", tag="acc")
+            for g in range(2):
+                i = 2 * b + g
+                for c in range(4):
+                    nc.tensor.matmul_mx(
+                        out=acc[:, g, :],
+                        lhsT=xq[:, i, c * P : (c + 1) * P].bitcast(FP8X4),
+                        lhsT_scale=xs[:, i, c * P : (c + 1) * P],
+                        rhs=wq[:, j, c, :].bitcast(FP8X4),
+                        rhs_scale=ws[:, j, c, :],
+                        start=(c == 0),
+                        stop=(c == 3),
+                    )
+            n = j // 2
+            if ("ost", n) not in st:
+                st[("ost", n)] = work.tile([P, 8, 512], F32, name="ost", tag="ost", bufs=2)
+            ost = st[("ost", n)]
+            o0 = (j % 2) * 256
+            nc.scalar.copy(out=ost[:, 2 * b : 2 * b + 2, o0 : o0 + 256], in_=acc[:])
+            if j % 2 == 1:
+                nc.sync.dma_start(
+                    out=of[2 * b * P : (2 * b + 2) * P, n * 512 : (n + 1) * 512].rearrange("(t p) o -> p t o", p=P),
+                    in_=ost[:, 2 * b : 2 * b + 2, :],
+                )
+
+        def x_one(i):
+            trans_x(i)
+            exit_x(i)
+
+        def x_pair(p):
+            trans_x(2 * p)
+            trans_x(2 * p + 1)
+            exit_x(2 * p)
+            exit_x(2 * p + 1)
+
+        def w_pair(j):
+            trans_w(2 * j)
+            trans_w(2 * j + 1)
+            exit_w(2 * j)
+            exit_w(2 * j + 1)
+
+        load_w(0)
+        load_scales()
+        load_x(0)
+        load_w(1)
+        load_x(1)
+        load_x(2)
+        load_x(3)
+        load_w(2)
+        load_w(3)
+        for i in range(4, 8):
+            load_x(i)
+        for t in range(4, 10):
+            load_w(t)
+
+        dup(0, 2)
+        sign_v([0])
+        mult(0)
+        trans_w(0)
+        exit_w(0)
+        x_one(0)
+        sign_v([1])
+        mult(1)
+        load_w(10)
+        load_w(11)
+        trans_w(1)
+        exit_w(1)
+        x_one(1)
+        quant_x(0)
+        quant_w(0)
+        quant_x(1)
+        x_pair(1)
+        dup(2, 16)
+        sign_v([2, 3])
+        mx_bank(0, 0)
+        quant_x(2)
+        quant_x(3)
+        x_pair(2)
+        mult(2)
+        mult(3)
+        load_w(12)
+        load_w(13)
+        mx_bank(0, 1)
+        quant_x(4)
+        quant_x(5)
+        x_pair(3)
+        mx_bank(0, 2)
+        w_pair(1)
+        sign_v([4, 5])
+        quant_x(6)
+        quant_x(7)
+        mx_bank(0, 3)
+        quant_w(1)
+        mult(4)
+        mult(5)
+        load_w(14)
+        load_w(15)
+        for j in range(1, 8):
+            for b in range(4):
+                if b == 2:
+                    if j + 1 < 8:
+                        w_pair(j + 1)
+                    if j + 2 < 8:
+                        sign_v([2 * j + 4, 2 * j + 5])
+                mx_bank(j, b)
+            if j + 1 < 8:
+                quant_w(j + 1)
+            if j + 2 < 8:
+                mult(2 * j + 4)
+                mult(2 * j + 5)

@@ -9,6 +9,7 @@ U32 = mybir.dt.uint32
 U8 = mybir.dt.uint8
 FP8X4 = mybir.dt.float8_e4m3fn_x4
 ALU = mybir.AluOpType
+ACT = mybir.ActivationFunctionType
 
 P = 128
 M = 1024
@@ -21,6 +22,7 @@ PINNED = True
 TINY = 2.0 ** -126
 AMP = 2.0 ** 7
 BACK = 2.0 ** 126
+S_COLS = 1024
 
 
 def tile_stebitlinear_kernel(tc, x, sign_weights, scales, out):
@@ -47,10 +49,10 @@ def tile_stebitlinear_kernel(tc, x, sign_weights, scales, out):
 
         st = {}
 
-        def load_scales():
+        def load_scales(t0, t1):
             nc.sync.dma_start(
-                out=sc_raw[:].rearrange("p (t g) -> p t g", g=64),
-                in_=scales.rearrange("(t p g) -> p t g", p=P, g=64),
+                out=sc_raw[:, t0 * 64 : t1 * 64].rearrange("p (t g) -> p t g", g=64),
+                in_=scales[t0 * P * 64 : t1 * P * 64].rearrange("(t p g) -> p t g", p=P, g=64),
             )
 
         def dup(t0, t1):
@@ -78,6 +80,14 @@ def tile_stebitlinear_kernel(tc, x, sign_weights, scales, out):
                 v = swp[:].rearrange("p t k -> p (t k)")
             else:
                 v = swp[:, ts[0] % 2, :]
+            nc.vector.tensor_scalar(out=v, in0=v, scalar1=AMP, scalar2=TINY, op0=ALU.mult, op1=ALU.min)
+            nc.vector.tensor_scalar(out=v, in0=v, scalar1=-TINY, scalar2=BACK, op0=ALU.max, op1=ALU.mult)
+
+        def sign_pair(j, s_cols):
+            v = st[("swp", j)][:].rearrange("p t k -> p (t k)")
+            if s_cols > 0:
+                nc.scalar.activation(out=v[:, 2 * K - s_cols :], in_=v[:, 2 * K - s_cols :], func=ACT.Sign)
+            v = v[:, : 2 * K - s_cols]
             nc.vector.tensor_scalar(out=v, in0=v, scalar1=AMP, scalar2=TINY, op0=ALU.mult, op1=ALU.min)
             nc.vector.tensor_scalar(out=v, in0=v, scalar1=-TINY, scalar2=BACK, op0=ALU.max, op1=ALU.mult)
 
@@ -165,7 +175,12 @@ def tile_stebitlinear_kernel(tc, x, sign_weights, scales, out):
             ost = st[("ost", n)]
             o0 = (j % 2) * 256
             nc.scalar.copy(out=ost[:, 2 * b : 2 * b + 2, o0 : o0 + 256], in_=acc[:])
-            if j % 2 == 1:
+            if n == 3:
+                nc.sync.dma_start(
+                    out=of[2 * b * P : (2 * b + 2) * P, j * 256 : (j + 1) * 256].rearrange("(t p) o -> p t o", p=P),
+                    in_=ost[:, 2 * b : 2 * b + 2, o0 : o0 + 256],
+                )
+            elif j % 2 == 1:
                 nc.sync.dma_start(
                     out=of[2 * b * P : (2 * b + 2) * P, n * 512 : (n + 1) * 512].rearrange("(t p) o -> p t o", p=P),
                     in_=ost[:, 2 * b : 2 * b + 2, :],
@@ -188,55 +203,64 @@ def tile_stebitlinear_kernel(tc, x, sign_weights, scales, out):
             exit_w(2 * j + 1)
 
         load_w(0)
-        load_scales()
+        load_scales(0, 2)
         load_x(0)
         load_w(1)
         load_x(1)
-        load_x(2)
-        load_x(3)
+        load_scales(2, 16)
+        for i in range(2, 6):
+            load_x(i)
         load_w(2)
         load_w(3)
-        for i in range(4, 8):
-            load_x(i)
+        load_x(6)
+        load_x(7)
         for t in range(4, 10):
             load_w(t)
 
+        if S_COLS > 0:
+            warm = keep.tile([P, 1], F32, name="warm")
+            nc.vector.memset(warm[:], 0.0)
+            nc.scalar.activation(out=warm[:], in_=warm[:], func=ACT.Sign)
         dup(0, 2)
         sign_v([0])
         mult(0)
+        x_one(0)
         trans_w(0)
         exit_w(0)
-        x_one(0)
         sign_v([1])
         mult(1)
         load_w(10)
         load_w(11)
+        x_one(1)
         trans_w(1)
         exit_w(1)
-        x_one(1)
         quant_x(0)
-        quant_w(0)
+        x_one(2)
         quant_x(1)
-        x_pair(1)
-        dup(2, 16)
-        sign_v([2, 3])
-        mx_bank(0, 0)
+        quant_w(0)
+        x_one(3)
         quant_x(2)
+        dup(2, 4)
+        x_one(4)
         quant_x(3)
-        x_pair(2)
+        x_one(5)
+        sign_pair(1, 0)
+        quant_x(4)
+        x_one(6)
+        quant_x(5)
         mult(2)
+        x_one(7)
         mult(3)
         load_w(12)
         load_w(13)
-        mx_bank(0, 1)
-        quant_x(4)
-        quant_x(5)
-        x_pair(3)
-        mx_bank(0, 2)
-        w_pair(1)
-        sign_v([4, 5])
         quant_x(6)
         quant_x(7)
+        mx_bank(0, 0)
+        mx_bank(0, 1)
+        w_pair(1)
+        dup(4, 6)
+        sign_pair(2, S_COLS)
+        mx_bank(0, 2)
         mx_bank(0, 3)
         quant_w(1)
         mult(4)
@@ -249,7 +273,8 @@ def tile_stebitlinear_kernel(tc, x, sign_weights, scales, out):
                     if j + 1 < 8:
                         w_pair(j + 1)
                     if j + 2 < 8:
-                        sign_v([2 * j + 4, 2 * j + 5])
+                        dup(2 * j + 4, 2 * j + 6)
+                        sign_pair(j + 2, S_COLS)
                 mx_bank(j, b)
             if j + 1 < 8:
                 quant_w(j + 1)

@@ -255,29 +255,19 @@ def tile_stebitlinear_kernel(tc, x, sign_weights, scales, out):
         load_w(13)
         quant_x(6)
         quant_x(7)
-        mx_bank(0, 0)
-        mx_bank(0, 1)
-        w_pair(1)
-        dup(4, 6)
-        sign_pair(2, S_COLS)
-        mx_bank(0, 2)
-        mx_bank(0, 3)
-        quant_w(1)
-        mult(4)
-        mult(5)
-        load_w(14)
-        load_w(15)
-        for j in range(1, 8):
+        for j in range(8):
             for b in range(4):
-                if b == 2:
-                    if j + 1 < 8:
-                        w_pair(j + 1)
+                if b == 1 and j + 1 < 8:
+                    w_pair(j + 1)
                     if j + 2 < 8:
                         dup(2 * j + 4, 2 * j + 6)
                         sign_pair(j + 2, S_COLS)
                 mx_bank(j, b)
-            if j + 1 < 8:
-                quant_w(j + 1)
-            if j + 2 < 8:
-                mult(2 * j + 4)
-                mult(2 * j + 5)
+                if b == 2 and j + 1 < 8:
+                    quant_w(j + 1)
+                    if j + 2 < 8:
+                        mult(2 * j + 4)
+                        mult(2 * j + 5)
+                    if j + 7 < 8:
+                        load_w(2 * j + 14)
+                        load_w(2 * j + 15)

@@ -203,17 +203,17 @@ def tile_stebitlinear_kernel(tc, x, sign_weights, scales, out):
             exit_w(2 * j + 1)
 
         load_w(0)
-        load_scales(0, 2)
+        load_scales(0, 4)
         load_x(0)
         load_w(1)
         load_x(1)
-        load_scales(2, 16)
         for i in range(2, 6):
             load_x(i)
         load_w(2)
         load_w(3)
         load_x(6)
         load_x(7)
+        load_scales(4, 16)
         for t in range(4, 10):
             load_w(t)
 

@@ -244,7 +244,7 @@ def tile_stebitlinear_kernel(tc, x, sign_weights, scales, out):
         x_one(4)
         quant_x(3)
         x_one(5)
-        sign_pair(1, 0)
+        sign_pair(1, S_COLS)
         quant_x(4)
         x_one(6)
         quant_x(5)

@@ -91,6 +91,16 @@ def tile_stebitlinear_kernel(tc, x, sign_weights, scales, out):
             nc.vector.tensor_scalar(out=v, in0=v, scalar1=AMP, scalar2=TINY, op0=ALU.mult, op1=ALU.min)
             nc.vector.tensor_scalar(out=v, in0=v, scalar1=-TINY, scalar2=BACK, op0=ALU.max, op1=ALU.mult)
 
+        def sign_pair_first(j, s_cols):
+            v = st[("swp", j)][:].rearrange("p t k -> p (t k)")
+            nc.scalar.activation(out=v[:, 2 * K - s_cols :], in_=v[:, 2 * K - s_cols :], func=ACT.Sign)
+            v = v[:, : 2 * K - s_cols]
+            nc.vector.tensor_scalar(out=v, in0=v, scalar1=AMP, scalar2=TINY, op0=ALU.mult, op1=ALU.min)
+
+        def sign_pair_second(j, s_cols):
+            v = st[("swp", j)][:].rearrange("p t k -> p (t k)")[:, : 2 * K - s_cols]
+            nc.vector.tensor_scalar(out=v, in0=v, scalar1=-TINY, scalar2=BACK, op0=ALU.max, op1=ALU.mult)
+
         def mult(t):
             j = t // 2
             if ("wsr", j) not in st:
@@ -244,8 +254,9 @@ def tile_stebitlinear_kernel(tc, x, sign_weights, scales, out):
         x_one(4)
         quant_x(3)
         x_one(5)
-        sign_pair(1, S_COLS)
+        sign_pair_first(1, S_COLS)
         quant_x(4)
+        sign_pair_second(1, S_COLS)
         x_one(6)
         quant_x(5)
         mult(2)
@@ -261,7 +272,7 @@ def tile_stebitlinear_kernel(tc, x, sign_weights, scales, out):
                     w_pair(j + 1)
                     if j + 2 < 8:
                         dup(2 * j + 4, 2 * j + 6)
-                        sign_pair(j + 2, S_COLS)
+                        sign_pair(j + 2, S_COLS + 512 if j == 0 else S_COLS)
                 mx_bank(j, b)
                 if b == 2 and j + 1 < 8:
                     quant_w(j + 1)

@@ -49,6 +49,20 @@ def tile_stebitlinear_kernel(tc, x, sign_weights, scales, out):
 
         st = {}
 
+        wz = keep.tile([P, 512], BF16, name="wz")
+        nc.vector.memset(wz[:], 1.0)
+        dm = psum_m.tile([P, 2, 256], F32, name="acc", tag="acc")
+
+        def dummy(n):
+            for i in range(n):
+                nc.tensor.matmul(
+                    out=dm[:].rearrange("p a b -> p (a b)"),
+                    lhsT=wz[:, 0:P],
+                    rhs=wz[:],
+                    start=True,
+                    stop=True,
+                )
+
         def load_scales(t0, t1):
             nc.sync.dma_start(
                 out=sc_raw[:, t0 * 64 : t1 * 64].rearrange("p (t g) -> p t g", g=64),
@@ -257,9 +271,11 @@ def tile_stebitlinear_kernel(tc, x, sign_weights, scales, out):
         sign_pair_first(1, S_COLS)
         quant_x(4)
         sign_pair_second(1, S_COLS)
+        dummy(3)
         x_one(6)
         quant_x(5)
         mult(2)
+        dummy(2)
         x_one(7)
         mult(3)
         load_w(12)

@@ -231,12 +231,12 @@ def tile_stebitlinear_kernel(tc, x, sign_weights, scales, out):
         load_x(0)
         load_w(1)
         load_x(1)
-        for i in range(2, 6):
+        for i in range(2, 5):
             load_x(i)
         load_w(2)
         load_w(3)
-        load_x(6)
-        load_x(7)
+        for i in range(5, 8):
+            load_x(i)
         load_scales(4, 16)
         for t in range(4, 10):
             load_w(t)
@@ -266,20 +266,20 @@ def tile_stebitlinear_kernel(tc, x, sign_weights, scales, out):
         quant_x(2)
         dup(2, 4)
         x_one(4)
-        quant_x(3)
-        x_one(5)
         sign_pair_first(1, S_COLS)
-        quant_x(4)
+        quant_x(3)
         sign_pair_second(1, S_COLS)
+        x_one(5)
+        quant_x(4)
+        mult(2)
         dummy(3)
         x_one(6)
-        quant_x(5)
-        mult(2)
-        dummy(2)
-        x_one(7)
         mult(3)
         load_w(12)
         load_w(13)
+        quant_x(5)
+        dummy(2)
+        x_one(7)
         quant_x(6)
         quant_x(7)
         for j in range(8):

@@ -6,6 +6,7 @@ from concourse.masks import make_identity
 F32 = mybir.dt.float32
 BF16 = mybir.dt.bfloat16
 U32 = mybir.dt.uint32
+I32 = mybir.dt.int32
 U8 = mybir.dt.uint8
 FP8X4 = mybir.dt.float8_e4m3fn_x4
 ALU = mybir.AluOpType
@@ -19,10 +20,8 @@ FLOPS = 2 * M * K * O
 
 PINNED = True
 
-TINY = 2.0 ** -126
-AMP = 2.0 ** 7
-BACK = 2.0 ** 126
-S_COLS = 1024
+HUGE = 2.0 ** 127
+ONES = 0x03FF03FF
 
 
 def tile_stebitlinear_kernel(tc, x, sign_weights, scales, out):
@@ -71,9 +70,11 @@ def tile_stebitlinear_kernel(tc, x, sign_weights, scales, out):
 
         def dup(t0, t1):
             n = (t1 - t0) * 64
-            nc.scalar.copy(
+            nc.scalar.activation(
                 out=sc2[:, t0 * 64 : t1 * 64, :],
                 in_=sc_raw[:, t0 * 64 : t1 * 64].unsqueeze(2).to_broadcast([P, n, 2]),
+                func=ACT.Copy,
+                scale=-1.0,
             )
 
         def load_w(t):
@@ -94,38 +95,24 @@ def tile_stebitlinear_kernel(tc, x, sign_weights, scales, out):
                 v = swp[:].rearrange("p t k -> p (t k)")
             else:
                 v = swp[:, ts[0] % 2, :]
-            nc.vector.tensor_scalar(out=v, in0=v, scalar1=AMP, scalar2=TINY, op0=ALU.mult, op1=ALU.min)
-            nc.vector.tensor_scalar(out=v, in0=v, scalar1=-TINY, scalar2=BACK, op0=ALU.max, op1=ALU.mult)
-
-        def sign_pair(j, s_cols):
-            v = st[("swp", j)][:].rearrange("p t k -> p (t k)")
-            if s_cols > 0:
-                nc.scalar.activation(out=v[:, 2 * K - s_cols :], in_=v[:, 2 * K - s_cols :], func=ACT.Sign)
-            v = v[:, : 2 * K - s_cols]
-            nc.vector.tensor_scalar(out=v, in0=v, scalar1=AMP, scalar2=TINY, op0=ALU.mult, op1=ALU.min)
-            nc.vector.tensor_scalar(out=v, in0=v, scalar1=-TINY, scalar2=BACK, op0=ALU.max, op1=ALU.mult)
-
-        def sign_pair_first(j, s_cols):
-            v = st[("swp", j)][:].rearrange("p t k -> p (t k)")
-            nc.scalar.activation(out=v[:, 2 * K - s_cols :], in_=v[:, 2 * K - s_cols :], func=ACT.Sign)
-            v = v[:, : 2 * K - s_cols]
-            nc.vector.tensor_scalar(out=v, in0=v, scalar1=AMP, scalar2=TINY, op0=ALU.mult, op1=ALU.min)
-
-        def sign_pair_second(j, s_cols):
-            v = st[("swp", j)][:].rearrange("p t k -> p (t k)")[:, : 2 * K - s_cols]
-            nc.vector.tensor_scalar(out=v, in0=v, scalar1=-TINY, scalar2=BACK, op0=ALU.max, op1=ALU.mult)
+            nc.vector.tensor_scalar(out=v, in0=v, scalar1=HUGE, scalar2=HUGE, op0=ALU.mult, op1=ALU.mult)
 
         def mult(t):
             j = t // 2
             if ("wsr", j) not in st:
                 st[("wsr", j)] = work.tile([P, 2 * K], BF16, name="wsr", tag="wsr", bufs=2)
-            wsr = st[("wsr", j)]
-            nc.vector.tensor_tensor(
-                out=wsr[:].rearrange("p (t u q e) -> p t q u e", t=2, u=2, q=512, e=2)[:, t % 2],
-                in0=st[("swp", j)][:, t % 2, :],
-                in1=sc2[:, t * 64 : (t + 1) * 64, :].unsqueeze(2).to_broadcast([P, 64, 16, 2]),
-                op=ALU.mult,
-            )
+            wsr = st[("wsr", j)][:].bitcast(I32).rearrange("p (t u g r) -> p t u g r", t=2, u=2, r=8)
+            words = st[("swp", j)][:, t % 2, :].bitcast(I32).rearrange("p (g r u) -> p u g r", u=2, r=8)
+            mag = sc2[:, t * 64 : (t + 1) * 64, :].rearrange("p g e -> p (g e)").bitcast(I32)
+            for u in range(2):
+                nc.vector.scalar_tensor_tensor(
+                    out=wsr[:, t % 2, u],
+                    in0=words[:, u],
+                    scalar=ONES,
+                    in1=mag.unsqueeze(2).to_broadcast([P, 64, 8]),
+                    op0=ALU.bitwise_or,
+                    op1=ALU.bitwise_and,
+                )
 
         def trans_w(t):
             words = st[("wsr", t // 2)][:].bitcast(F32).rearrange("p (t u c q) -> p t u c q", t=2, u=2, c=4)
@@ -241,10 +228,6 @@ def tile_stebitlinear_kernel(tc, x, sign_weights, scales, out):
         for t in range(4, 10):
             load_w(t)
 
-        if S_COLS > 0:
-            warm = keep.tile([P, 1], F32, name="warm")
-            nc.vector.memset(warm[:], 0.0)
-            nc.scalar.activation(out=warm[:], in_=warm[:], func=ACT.Sign)
         dup(0, 2)
         sign_v([0])
         mult(0)
@@ -266,9 +249,8 @@ def tile_stebitlinear_kernel(tc, x, sign_weights, scales, out):
         quant_x(2)
         dup(2, 4)
         x_one(4)
-        sign_pair_first(1, S_COLS)
+        sign_v([2, 3])
         quant_x(3)
-        sign_pair_second(1, S_COLS)
         x_one(5)
         quant_x(4)
         mult(2)
@@ -288,7 +270,7 @@ def tile_stebitlinear_kernel(tc, x, sign_weights, scales, out):
                     w_pair(j + 1)
                     if j + 2 < 8:
                         dup(2 * j + 4, 2 * j + 6)
-                        sign_pair(j + 2, S_COLS + 512 if j == 0 else S_COLS)
+                        sign_v([2 * j + 4, 2 * j + 5])
                 mx_bank(j, b)
                 if b == 2 and j + 1 < 8:
                     quant_w(j + 1)

@@ -64,8 +64,8 @@ def tile_stebitlinear_kernel(tc, x, sign_weights, scales, out):
 
         def load_scales(t0, t1):
             nc.sync.dma_start(
-                out=sc_raw[:, t0 * 64 : t1 * 64].rearrange("p (t g) -> p t g", g=64),
-                in_=scales[t0 * P * 64 : t1 * P * 64].rearrange("(t p g) -> p t g", p=P, g=64),
+                out=sc_raw[:, t0 * 64 : t1 * 64].rearrange("p (j c) -> p j c", c=128),
+                in_=scales[t0 * P * 64 : t1 * P * 64].rearrange("(j p c) -> p j c", p=P, c=128),
             )
 
         def dup(t0, t1):
@@ -77,17 +77,31 @@ def tile_stebitlinear_kernel(tc, x, sign_weights, scales, out):
                 scale=-1.0,
             )
 
-        def load_w(t):
-            j = t // 2
+        def w_rows(j):
             if ("swp", j) not in st:
                 st[("swp", j)] = work.tile([P, 2, K], BF16, name="swp", tag="swp", bufs=5)
-            nc.sync.dma_start(out=st[("swp", j)][:, t % 2, :], in_=sign_weights[t * P : (t + 1) * P, :])
+            return st[("swp", j)], sign_weights[2 * j * P : (2 * j + 2) * P, :].rearrange("(p t) k -> p t k", t=2)
+
+        def load_w(t):
+            tile, rows = w_rows(t // 2)
+            nc.sync.dma_start(out=tile[:, t % 2, :], in_=rows[:, t % 2, :])
+
+        def load_w_pair(j):
+            tile, rows = w_rows(j)
+            nc.sync.dma_start(out=tile[:], in_=rows)
+
+        def x_rows(b):
+            if ("xr", b) not in st:
+                st[("xr", b)] = work.tile([P, 2, K], BF16, name="xr", tag="xr", bufs=4)
+            return st[("xr", b)], xf[2 * b * P : (2 * b + 2) * P, :].rearrange("(p t) k -> p t k", t=2)
 
         def load_x(i):
-            j = i // 2
-            if ("xr", j) not in st:
-                st[("xr", j)] = work.tile([P, 2, K], BF16, name="xr", tag="xr", bufs=4)
-            nc.sync.dma_start(out=st[("xr", j)][:, i % 2, :], in_=xf[i * P : (i + 1) * P, :])
+            tile, rows = x_rows(i // 2)
+            nc.sync.dma_start(out=tile[:, i % 2, :], in_=rows[:, i % 2, :])
+
+        def load_x_pair(b):
+            tile, rows = x_rows(b)
+            nc.sync.dma_start(out=tile[:], in_=rows)
 
         def sign_v(ts):
             swp = st[("swp", ts[0] // 2)]
@@ -185,15 +199,18 @@ def tile_stebitlinear_kernel(tc, x, sign_weights, scales, out):
                 st[("ost", n)] = work.tile([P, 8, 512], F32, name="ost", tag="ost", bufs=2)
             ost = st[("ost", n)]
             o0 = (j % 2) * 256
-            nc.scalar.copy(out=ost[:, 2 * b : 2 * b + 2, o0 : o0 + 256], in_=acc[:])
+            nc.scalar.copy(
+                out=ost[:, 2 * b : 2 * b + 2, o0 : o0 + 256].rearrange("p g (q t) -> p g q t", t=2),
+                in_=acc[:].rearrange("p g (t q) -> p g q t", t=2),
+            )
             if n == 3:
                 nc.sync.dma_start(
-                    out=of[2 * b * P : (2 * b + 2) * P, j * 256 : (j + 1) * 256].rearrange("(t p) o -> p t o", p=P),
+                    out=of[2 * b * P : (2 * b + 2) * P, j * 256 : (j + 1) * 256].rearrange("(p t) o -> p t o", t=2),
                     in_=ost[:, 2 * b : 2 * b + 2, o0 : o0 + 256],
                 )
             elif j % 2 == 1:
                 nc.sync.dma_start(
-                    out=of[2 * b * P : (2 * b + 2) * P, n * 512 : (n + 1) * 512].rearrange("(t p) o -> p t o", p=P),
+                    out=of[2 * b * P : (2 * b + 2) * P, n * 512 : (n + 1) * 512].rearrange("(p t) o -> p t o", t=2),
                     in_=ost[:, 2 * b : 2 * b + 2, :],
                 )
 
@@ -218,15 +235,14 @@ def tile_stebitlinear_kernel(tc, x, sign_weights, scales, out):
         load_x(0)
         load_w(1)
         load_x(1)
-        for i in range(2, 5):
-            load_x(i)
-        load_w(2)
-        load_w(3)
-        for i in range(5, 8):
-            load_x(i)
+        load_x_pair(1)
+        load_x(4)
+        load_w_pair(1)
+        load_x(5)
+        load_x_pair(3)
         load_scales(4, 16)
-        for t in range(4, 10):
-            load_w(t)
+        for j in range(2, 5):
+            load_w_pair(j)
 
         dup(0, 2)
         sign_v([0])
@@ -236,8 +252,7 @@ def tile_stebitlinear_kernel(tc, x, sign_weights, scales, out):
         exit_w(0)
         sign_v([1])
         mult(1)
-        load_w(10)
-        load_w(11)
+        load_w_pair(5)
         x_one(1)
         trans_w(1)
         exit_w(1)
@@ -257,8 +272,7 @@ def tile_stebitlinear_kernel(tc, x, sign_weights, scales, out):
         dummy(3)
         x_one(6)
         mult(3)
-        load_w(12)
-        load_w(13)
+        load_w_pair(6)
         quant_x(5)
         dummy(2)
         x_one(7)
@@ -278,5 +292,4 @@ def tile_stebitlinear_kernel(tc, x, sign_weights, scales, out):
                         mult(2 * j + 4)
                         mult(2 * j + 5)
                     if j + 7 < 8:
-                        load_w(2 * j + 14)
-                        load_w(2 * j + 15)
+                        load_w_pair(j + 7)

@@ -99,10 +99,6 @@ def tile_stebitlinear_kernel(tc, x, sign_weights, scales, out):
             tile, rows = x_rows(i // 2)
             nc.sync.dma_start(out=tile[:, i % 2, :], in_=rows[:, i % 2, :])
 
-        def load_x_pair(b):
-            tile, rows = x_rows(b)
-            nc.sync.dma_start(out=tile[:], in_=rows)
-
         def sign_v(ts):
             swp = st[("swp", ts[0] // 2)]
             if len(ts) == 2:
@@ -235,16 +231,12 @@ def tile_stebitlinear_kernel(tc, x, sign_weights, scales, out):
         load_x(0)
         load_w(1)
         load_x(1)
-        load_x_pair(1)
-        load_x(4)
+        for i in range(2, 6): load_x(i)
         load_w_pair(1)
-        load_x(5)
-        load_x_pair(3)
+        for i in range(6, 8): load_x(i)
         load_scales(4, 16)
-        for j in range(2, 5):
-            load_w_pair(j)
-
-        dup(0, 2)
+        for j in range(2, 5): load_w_pair(j)
+        dup(0, 4)
         sign_v([0])
         mult(0)
         x_one(0)
@@ -262,18 +254,17 @@ def tile_stebitlinear_kernel(tc, x, sign_weights, scales, out):
         quant_w(0)
         x_one(3)
         quant_x(2)
-        dup(2, 4)
         x_one(4)
-        sign_v([2, 3])
         quant_x(3)
         x_one(5)
+        sign_v([2, 3])
         quant_x(4)
         mult(2)
         dummy(3)
         x_one(6)
+        quant_x(5)
         mult(3)
         load_w_pair(6)
-        quant_x(5)
         dummy(2)
         x_one(7)
         quant_x(6)

from contextlib import ExitStack

import concourse.mybir as mybir
from concourse.masks import make_identity

F32 = mybir.dt.float32
BF16 = mybir.dt.bfloat16
U32 = mybir.dt.uint32
I32 = mybir.dt.int32
U8 = mybir.dt.uint8
FP8X4 = mybir.dt.float8_e4m3fn_x4
ALU = mybir.AluOpType
ACT = mybir.ActivationFunctionType

P = 128
M = 1024
K = 2048
O = 2048
FLOPS = 2 * M * K * O

PINNED = True

HUGE = 2.0 ** 127
ONES = 0x03FF03FF


def tile_stebitlinear_kernel(tc, x, sign_weights, scales, out):
    nc = tc.nc
    xf = x.flatten_outer_dims()
    of = out.flatten_outer_dims()
    with ExitStack() as ctx:
        keep = ctx.enter_context(tc.tile_pool(name="keep", bufs=1))
        work = ctx.enter_context(tc.tile_pool(name="work", bufs=2))
        psum_t = ctx.enter_context(tc.psum_pool(name="psum_t", bufs=4))
        psum_m = ctx.enter_context(tc.psum_pool(name="psum_m", bufs=4))

        ident = keep.tile([P, P], F32, name="ident")
        make_identity(nc, ident[:])
        sc_raw = keep.tile([P, 16 * 64], BF16, name="sc_raw")
        sc2 = keep.tile([P, 16 * 64, 2], BF16, name="sc2")
        xq = keep.tile([P, 8, 512], U32, name="xq", align_bytes=64)
        xs = keep.tile([P, 8, 512], U8, name="xs", align_bytes=64)
        wq = keep.tile([P, 8, 4, 256], U32, name="wq", align_bytes=64)
        ws = keep.tile([P, 8, 4, 256], U8, name="ws", align_bytes=64)

        if PINNED:
            ctx.enter_context(tc.manual_schedule())

        st = {}

        wz = keep.tile([P, 512], BF16, name="wz")
        nc.vector.memset(wz[:], 1.0)
        dm = psum_m.tile([P, 2, 256], F32, name="acc", tag="acc")

        def dummy(n):
            for i in range(n):
                nc.tensor.matmul(
                    out=dm[:].rearrange("p a b -> p (a b)"),
                    lhsT=wz[:, 0:P],
                    rhs=wz[:],
                    start=True,
                    stop=True,
                )

        def load_scales(t0, t1):
            nc.sync.dma_start(
                out=sc_raw[:, t0 * 64 : t1 * 64].rearrange("p (j c) -> p j c", c=128),
                in_=scales[t0 * P * 64 : t1 * P * 64].rearrange("(j p c) -> p j c", p=P, c=128),
            )

        def dup(t0, t1):
            n = (t1 - t0) * 64
            nc.scalar.activation(
                out=sc2[:, t0 * 64 : t1 * 64, :],
                in_=sc_raw[:, t0 * 64 : t1 * 64].unsqueeze(2).to_broadcast([P, n, 2]),
                func=ACT.Copy,
                scale=-1.0,
            )

        def w_rows(j):
            if ("swp", j) not in st:
                st[("swp", j)] = work.tile([P, 2, K], BF16, name="swp", tag="swp", bufs=5)
            return st[("swp", j)], sign_weights[2 * j * P : (2 * j + 2) * P, :].rearrange("(p t) k -> p t k", t=2)

        def load_w(t):
            tile, rows = w_rows(t // 2)
            nc.sync.dma_start(out=tile[:, t % 2, :], in_=rows[:, t % 2, :])

        def load_w_pair(j):
            tile, rows = w_rows(j)
            nc.sync.dma_start(out=tile[:], in_=rows)

        def x_rows(b):
            if ("xr", b) not in st:
                st[("xr", b)] = work.tile([P, 2, K], BF16, name="xr", tag="xr", bufs=4)
            return st[("xr", b)], xf[2 * b * P : (2 * b + 2) * P, :].rearrange("(p t) k -> p t k", t=2)

        def load_x(i):
            tile, rows = x_rows(i // 2)
            nc.sync.dma_start(out=tile[:, i % 2, :], in_=rows[:, i % 2, :])

        def sign_v(ts):
            swp = st[("swp", ts[0] // 2)]
            if len(ts) == 2:
                v = swp[:].rearrange("p t k -> p (t k)")
            else:
                v = swp[:, ts[0] % 2, :]
            nc.vector.tensor_scalar(out=v, in0=v, scalar1=HUGE, scalar2=HUGE, op0=ALU.mult, op1=ALU.mult)

        def mult(t):
            j = t // 2
            if ("wsr", j) not in st:
                st[("wsr", j)] = work.tile([P, 2 * K], BF16, name="wsr", tag="wsr", bufs=2)
            wsr = st[("wsr", j)][:].bitcast(I32).rearrange("p (t u g r) -> p t u g r", t=2, u=2, r=8)
            words = st[("swp", j)][:, t % 2, :].bitcast(I32).rearrange("p (g r u) -> p u g r", u=2, r=8)
            mag = sc2[:, t * 64 : (t + 1) * 64, :].rearrange("p g e -> p (g e)").bitcast(I32)
            for u in range(2):
                nc.vector.scalar_tensor_tensor(
                    out=wsr[:, t % 2, u],
                    in0=words[:, u],
                    scalar=ONES,
                    in1=mag.unsqueeze(2).to_broadcast([P, 64, 8]),
                    op0=ALU.bitwise_or,
                    op1=ALU.bitwise_and,
                )

        def trans_w(t):
            words = st[("wsr", t // 2)][:].bitcast(F32).rearrange("p (t u c q) -> p t u c q", t=2, u=2, c=4)
            for h in range(2):
                tp = psum_t.tile([P, 2, 2, P], F32, name="tp", tag="tp")
                st[("tpw", t, h)] = tp
                for cc in range(2):
                    for u in range(2):
                        nc.tensor.transpose(tp[:, cc, u, :], words[:, t % 2, u, 2 * h + cc, :], ident[:])

        def exit_w(t):
            j = t // 2
            if ("wg", j) not in st:
                st[("wg", j)] = work.tile([P, 2 * K], BF16, name="wg", tag="wg", bufs=2, align_bytes=64)
            words = st[("wg", j)][:].bitcast(F32).rearrange("p (c o u) -> p c o u", c=4, u=2)
            o0 = (t % 2) * P
            for h in range(2):
                nc.scalar.copy(
                    out=words[:, 2 * h : 2 * h + 2, o0 : o0 + P, :],
                    in_=st[("tpw", t, h)][:].rearrange("p c u m -> p c m u"),
                )

        def quant_w(j):
            wg = st[("wg", j)]
            for c in range(4):
                nc.vector.quantize_mx(
                    out=wq[:, j, c, :].bitcast(FP8X4),
                    scales=ws[:, j, c, :],
                    in_=wg[:, c * 1024 : (c + 1) * 1024],
                )

        def trans_x(i):
            words = st[("xr", i // 2)][:].bitcast(F32).rearrange("p t (c q u) -> p t c u q", c=4, u=2)
            for h in range(2):
                tp = psum_t.tile([P, 2, 2, P], F32, name="tp", tag="tp")
                st[("tpx", i, h)] = tp
                for cc in range(2):
                    for u in range(2):
                        nc.tensor.transpose(tp[:, cc, u, :], words[:, i % 2, 2 * h + cc, u, :], ident[:])

        def exit_x(i):
            xg = work.tile([P, K], BF16, name="xg", tag="xg", bufs=4, align_bytes=64)
            st[("xg", i)] = xg
            words = xg[:].bitcast(F32).rearrange("p (c m u) -> p c m u", c=4, u=2)
            for h in range(2):
                nc.scalar.copy(
                    out=words[:, 2 * h : 2 * h + 2, :, :],
                    in_=st[("tpx", i, h)][:].rearrange("p c u m -> p c m u"),
                )

        def quant_x(i):
            nc.vector.quantize_mx(out=xq[:, i, :].bitcast(FP8X4), scales=xs[:, i, :], in_=st[("xg", i)][:])

        def mx_bank(j, b):
            acc = psum_m.tile([P, 2, 256], F32, name="acc", tag="acc")
            for g in range(2):
                i = 2 * b + g
                for c in range(4):
                    nc.tensor.matmul_mx(
                        out=acc[:, g, :],
                        lhsT=xq[:, i, c * P : (c + 1) * P].bitcast(FP8X4),
                        lhsT_scale=xs[:, i, c * P : (c + 1) * P],
                        rhs=wq[:, j, c, :].bitcast(FP8X4),
                        rhs_scale=ws[:, j, c, :],
                        start=(c == 0),
                        stop=(c == 3),
                    )
            n = j // 2
            if ("ost", n) not in st:
                st[("ost", n)] = work.tile([P, 8, 512], F32, name="ost", tag="ost", bufs=2)
            ost = st[("ost", n)]
            o0 = (j % 2) * 256
            nc.scalar.copy(
                out=ost[:, 2 * b : 2 * b + 2, o0 : o0 + 256].rearrange("p g (q t) -> p g q t", t=2),
                in_=acc[:].rearrange("p g (t q) -> p g q t", t=2),
            )
            if n == 3:
                nc.sync.dma_start(
                    out=of[2 * b * P : (2 * b + 2) * P, j * 256 : (j + 1) * 256].rearrange("(p t) o -> p t o", t=2),
                    in_=ost[:, 2 * b : 2 * b + 2, o0 : o0 + 256],
                )
            elif j % 2 == 1:
                nc.sync.dma_start(
                    out=of[2 * b * P : (2 * b + 2) * P, n * 512 : (n + 1) * 512].rearrange("(p t) o -> p t o", t=2),
                    in_=ost[:, 2 * b : 2 * b + 2, :],
                )

        def x_one(i):
            trans_x(i)
            exit_x(i)

        def x_pair(p):
            trans_x(2 * p)
            trans_x(2 * p + 1)
            exit_x(2 * p)
            exit_x(2 * p + 1)

        def w_pair(j):
            trans_w(2 * j)
            trans_w(2 * j + 1)
            exit_w(2 * j)
            exit_w(2 * j + 1)

        load_w(0)
        load_scales(0, 4)
        load_x(0)
        load_w(1)
        load_x(1)
        for i in range(2, 6): load_x(i)
        load_w_pair(1)
        for i in range(6, 8): load_x(i)
        load_scales(4, 16)
        for j in range(2, 5): load_w_pair(j)
        dup(0, 4)
        sign_v([0])
        mult(0)
        x_one(0)
        trans_w(0)
        exit_w(0)
        sign_v([1])
        mult(1)
        load_w_pair(5)
        x_one(1)
        trans_w(1)
        exit_w(1)
        quant_x(0)
        x_one(2)
        quant_x(1)
        quant_w(0)
        x_one(3)
        quant_x(2)
        x_one(4)
        quant_x(3)
        x_one(5)
        sign_v([2, 3])
        quant_x(4)
        mult(2)
        dummy(3)
        x_one(6)
        quant_x(5)
        mult(3)
        load_w_pair(6)
        dummy(2)
        x_one(7)
        quant_x(6)
        quant_x(7)
        for j in range(8):
            for b in range(4):
                if b == 1 and j + 1 < 8:
                    w_pair(j + 1)
                    if j + 2 < 8:
                        dup(2 * j + 4, 2 * j + 6)
                        sign_v([2 * j + 4, 2 * j + 5])
                mx_bank(j, b)
                if b == 2 and j + 1 < 8:
                    quant_w(j + 1)
                    if j + 2 < 8:
                        mult(2 * j + 4)
                        mult(2 * j + 5)
                    if j + 7 < 8:
                        load_w_pair(j + 7)
